import numpy as np
import ml_dtypes


def mxq(x, axis, fmt="e4m3"):
    dtype, down = {"e4m3": (ml_dtypes.float8_e4m3fn, 7), "e5m2": (ml_dtypes.float8_e5m2, 14)}[fmt]
    v = np.moveaxis(np.asarray(x, np.float32).astype(ml_dtypes.bfloat16).astype(np.float64), axis, -1)
    blocks = v.reshape(v.shape[:-1] + (-1, 32))
    amax = np.abs(blocks).max(-1, keepdims=True)
    byte = np.maximum(np.where(amax > 0, np.frexp(amax)[1] - 1 + 127, 0) - down, 1)
    scale = np.exp2(byte - 127.0)
    codes = (blocks / scale).astype(np.float32).astype(dtype).astype(np.float64)
    return np.moveaxis((codes * scale).reshape(v.shape), -1, axis)


WIDE = False


def mx_kscale(k):
    if not WIDE:
        return np.ones(k)
    levels = np.array([10, -10, 5, -5, 0])
    if k % 512:
        return np.exp2(np.random.permutation(np.resize(levels, k // 32))).repeat(32)
    a = np.empty((k // 512, 16))
    for p in range(k // 512):
        a[p, :8] = np.random.permutation(np.resize(levels, 8))
        for g in range(8):
            far = levels[np.abs(levels - a[p, g]) >= 10]
            a[p, g + 8] = far[np.random.randint(len(far))]
    return np.exp2(a.ravel()).repeat(32)


BF16 = ml_dtypes.bfloat16


def bf(x):
    return np.asarray(x, np.float32).astype(BF16)


def f64(x):
    return np.asarray(x).astype(np.float64)


T, B, D_IN, D_H, D_K, D_OUT = 8, 2048, 768, 1536, 1536, 384


def setup_inputs():
    s, t = mx_kscale(D_H), mx_kscale(D_K)
    return {"h1": bf(np.maximum(np.random.standard_normal((T, B, D_H)), 0.0) * s),
            "W2": bf(np.random.standard_normal((T, D_H, D_K)) * 1.4 / np.sqrt(D_H) / s[:, None] * t),
            "b2": bf(np.random.standard_normal((T, D_K)) * 0.2 * t),
            "W3": bf(np.random.standard_normal((T, D_K, D_OUT)) * 1.4 / np.sqrt(D_K) / t[:, None]),
            "b3": bf(np.random.standard_normal((T, D_OUT)) * 0.2)}


def reference(h1, W2, b2, W3, b3):
    h2 = np.maximum((mxq(f64(h1), 2, "e4m3") @ mxq(f64(W2), 1, "e4m3")) + f64(b2)[:, None, :], 0.0)
    out = (mxq(h2, 2, "e4m3") @ mxq(f64(W3), 1, "e4m3")) + f64(b3)[:, None, :]
    return out.mean(axis=0)

@@ -1,0 +1,368 @@
+from contextlib import ExitStack
+
+import concourse.masks as masks
+import concourse.mybir as mybir
+
+TREES, TOK, DH, DK, DO = 8, 2048, 1536, 1536, 384
+FLOPS = 2 * TREES * TOK * (DH * DK + DK * DO)
+
+F32 = mybir.dt.float32
+BF16 = mybir.dt.bfloat16
+U32 = mybir.dt.uint32
+U8 = mybir.dt.uint8
+FP8X4 = mybir.dt.float8_e4m3fn_x4
+ACT = mybir.ActivationFunctionType
+ALU = mybir.AluOpType
+
+P = 128
+BLK = 512
+NBLK = TOK // BLK
+STEPS = TREES * NBLK
+SLOTS = 3 * STEPS
+M0 = 80
+C0 = 240
+PRESORT = False
+
+
+def m2_of_slot(sig):
+    s, cg = divmod(sig, 3)
+    if sig < 3 or sig >= SLOTS or cg == 0:
+        return []
+    return [(s - 1, 2 * cg - 2), (s - 1, 2 * cg - 1)]
+
+
+def tr_of_slot(sig):
+    if sig == -1:
+        return [0, 1, 2]
+    if sig == 0:
+        return []
+    if sig == 1:
+        return [3, 4, 5]
+    if sig + 4 < SLOTS:
+        return [sig + 4]
+    return []
+
+
+def units_of_slot(sig):
+    if sig < 0:
+        return []
+    if sig == 0:
+        return [(0, i, True) for i in range(6)]
+    if sig == 1:
+        return [(0, i, True) for i in range(6, 9)]
+    if sig == 2:
+        return [(0, i, True) for i in range(9, 12)]
+    if sig < 6:
+        return [(1, 2 * (sig - 3), False), (1, 2 * (sig - 3) + 1, False)]
+    e, i = divmod(sig, 12)
+    if e + 1 < TREES:
+        return [(e + 1, i, False)]
+    return []
+
+
+def tile_randomforestmlp_pa_l_kernel(tc, h1, W2, b2, W3, b3, out):
+    nc = tc.nc
+    with ExitStack() as ctx:
+        const = ctx.enter_context(tc.tile_pool(name="const", bufs=1))
+        p_h1raw = ctx.enter_context(tc.tile_pool(name="h1raw", bufs=2))
+        p_h1g = ctx.enter_context(tc.tile_pool(name="h1g", bufs=3))
+        p_h1c = ctx.enter_context(tc.tile_pool(name="h1c", bufs=2))
+        p_wraw = ctx.enter_context(tc.tile_pool(name="wraw", bufs=6))
+        p_w3raw = ctx.enter_context(tc.tile_pool(name="w3raw", bufs=1))
+        p_wg = ctx.enter_context(tc.tile_pool(name="wg", bufs=4))
+        p_wc = ctx.enter_context(tc.tile_pool(name="wc", bufs=2))
+        p_h2b = ctx.enter_context(tc.tile_pool(name="h2b", bufs=3))
+        p_h2g = ctx.enter_context(tc.tile_pool(name="h2g", bufs=2))
+        p_h2c = ctx.enter_context(tc.tile_pool(name="h2c", bufs=2))
+        ps_m1 = ctx.enter_context(tc.psum_pool(name="psm1", bufs=4))
+        ps_tp = ctx.enter_context(tc.psum_pool(name="pstp", bufs=2))
+        ps_m2 = ctx.enter_context(tc.psum_pool(name="psm2", bufs=2))
+        ctx.enter_context(tc.manual_schedule())
+
+        ident = const.tile([P, P], F32, name="ident", tag="ident")
+        ones = const.tile([P, P], BF16, name="ones", tag="ones")
+        b3pad = const.tile([P, 512], BF16, name="b3pad", tag="b3pad")
+        b3m = const.tile([P, DO], F32, name="b3m", tag="b3m")
+        b2t = const.tile([P, TREES, 16], BF16, name="b2t", tag="b2t")
+        warm = const.tile([P, 8], F32, name="warm", tag="warm")
+        acc = const.tile([P, NBLK, 4, DO], F32, name="acc", tag="acc")
+
+        h1raw = {}
+        h1g = {}
+        h1c = {}
+        h1s = {}
+        wraw = {}
+        w3raw = {}
+        wg = {}
+        w2c = {}
+        w2s = {}
+        w3c = {}
+        w3s = {}
+        h2b = {}
+        h2g = {}
+        h2c = {}
+        h2s = {}
+        m2t = {}
+
+        def load_h1(s):
+            e, nb = divmod(s, NBLK)
+            t = p_h1raw.tile([P, 4, DH], BF16, name="h1raw", tag="h1raw")
+            h1raw[s] = t
+            nc.sync.dma_start(out=t[:], in_=h1[e, nb * BLK:(nb + 1) * BLK, :].rearrange("(p a) k -> p a k", a=4))
+
+        def load_w2(e, i):
+            cg, g = divmod(i, 3)
+            t = p_wraw.tile([P, 4, 512], BF16, name="wraw", tag="wraw")
+            wraw[(e, i)] = t
+            nc.sync.dma_start(
+                out=t[:],
+                in_=W2[e, 512 * g:512 * (g + 1), 512 * cg:512 * (cg + 1)].rearrange("(p j) c -> p j c", j=4),
+            )
+
+        def load_w3(e):
+            t = p_w3raw.tile([P, 3, 4, DO], BF16, name="w3raw", tag="w3raw")
+            w3raw[e] = t
+            nc.sync.dma_start(
+                out=t[:].rearrange("p g j c -> p g (j c)"),
+                in_=W3[e, :, :].rearrange("(g p j) c -> p g (j c)", g=3, j=4),
+            )
+
+        def load_b2(e):
+            nc.sync.dma_start(
+                out=b2t[:, e, 0:12].rearrange("p (c t) -> p c t", t=4),
+                in_=b2[e, :].rearrange("(c p t) -> p c t", c=3, t=4),
+            )
+
+        def tr_run(tau):
+            s, g = divmod(tau, 3)
+            words = h1raw[s][:].bitcast(F32)
+            hg = p_h1g.tile([P, 2048], BF16, name="h1g", tag="h1g", align_bytes=64)
+            h1g[tau] = hg
+            hgw = hg[:].bitcast(F32)
+            for b in range(2):
+                tp = ps_tp.tile([P, 2, 2, P], F32, name="tp", tag="tp")
+                for a2 in range(2):
+                    for u in range(2):
+                        nc.tensor.transpose(
+                            tp[:, a2, u, :], words[:, 2 * b + a2, 256 * g + u:256 * (g + 1):2], ident[:]
+                        )
+                nc.scalar.copy(
+                    out=hgw[:, 512 * b:512 * (b + 1)].rearrange("p (a r u) -> p a r u", a=2, u=2),
+                    in_=tp[:].rearrange("p a u r -> p a r u"),
+                )
+
+        def q1(tau):
+            s, g = divmod(tau, 3)
+            if g == 0:
+                hc = p_h1c.tile([P, 3, BLK], U32, name="h1c", tag="h1c", align_bytes=64)
+                hs = p_h1c.tile([P, 3, BLK], U8, name="h1s", tag="h1s", align_bytes=64)
+                h1c[s] = hc
+                h1s[s] = hs
+            nc.vector.quantize_mx(out=h1c[s][:, g, :].bitcast(FP8X4), scales=h1s[s][:, g, :], in_=h1g[tau][:])
+
+        def wg_of(u):
+            if u not in wg:
+                t = p_wg.tile([P, 2048], BF16, name="wg", tag="wg", align_bytes=64)
+                wg[u] = t
+            return wg[u]
+
+        def wc_views(u):
+            e, i = u
+            t = wg_of(u)
+            if i < 9:
+                dst = t[:].rearrange("p (t m j) -> p t m j", t=4, j=4)
+                src = wraw[u][:].rearrange("p j (m t) -> p t m j", t=4)
+                return (dst[:, :, 0:M0, :], src[:, :, 0:M0, :], dst[:, :, M0:P, :], src[:, :, M0:P, :])
+            dst = t[:, 0:4 * DO].rearrange("p (c j) -> p c j", j=4)
+            src = w3raw[e][:, i - 9, :, :].rearrange("p j c -> p c j")
+            return (dst[:, 0:C0, :], src[:, 0:C0, :], dst[:, C0:DO, :], src[:, C0:DO, :])
+
+        def wc_v(u):
+            v = wc_views(u)
+            nc.vector.tensor_copy(out=v[0], in_=v[1])
+
+        def wc_s(u):
+            v = wc_views(u)
+            nc.scalar.copy(out=v[2], in_=v[3])
+
+        def wq(u):
+            e, i = u
+            if i == 0:
+                a = p_wc.tile([P, 3, DK], U32, name="w2c", tag="w2c", align_bytes=64)
+                b = p_wc.tile([P, 3, DK], U8, name="w2s", tag="w2s", align_bytes=64)
+                w2c[e] = a
+                w2s[e] = b
+            if i == 9:
+                a = p_wc.tile([P, 3, DO], U32, name="w3c", tag="w3c", align_bytes=64)
+                b = p_wc.tile([P, 3, DO], U8, name="w3s", tag="w3s", align_bytes=64)
+                w3c[e] = a
+                w3s[e] = b
+            if i < 9:
+                cg, g = divmod(i, 3)
+                nc.vector.quantize_mx(
+                    out=w2c[e][:, g, 512 * cg:512 * (cg + 1)].bitcast(FP8X4),
+                    scales=w2s[e][:, g, 512 * cg:512 * (cg + 1)],
+                    in_=wg[u][:],
+                )
+            else:
+                g = i - 9
+                for (lo, hi) in ((0, 256), (256, 384)):
+                    nc.vector.quantize_mx(
+                        out=w3c[e][:, g, lo:hi].bitcast(FP8X4),
+                        scales=w3s[e][:, g, lo:hi],
+                        in_=wg[u][:, 4 * lo:4 * hi],
+                    )
+
+        def m1(sig):
+            s, cg = divmod(sig, 3)
+            e = s // NBLK
+            hb = p_h2b.tile([P, 4, BLK], BF16, name="h2b", tag="h2b")
+            h2b[sig] = hb
+            for t in range(4):
+                bank = ps_m1.tile([P, BLK], F32, name="m1", tag="m1")
+                c0 = 512 * cg + 128 * t
+                for g in range(3):
+                    nc.tensor.matmul_mx(
+                        out=bank[:],
+                        lhsT=w2c[e][:, g, c0:c0 + P].bitcast(FP8X4),
+                        lhsT_scale=w2s[e][:, g, c0:c0 + P],
+                        rhs=h1c[s][:, g, :].bitcast(FP8X4),
+                        rhs_scale=h1s[s][:, g, :],
+                        start=(g == 0),
+                        stop=(g == 2),
+                    )
+                nc.scalar.activation(
+                    out=hb[:, t, :], in_=bank[:], func=ACT.Relu,
+                    bias=b2t[:, e, 4 * cg + t:4 * cg + t + 1], scale=1.0,
+                )
+
+        def i2(sig):
+            hg = p_h2g.tile([P, BLK, 4], BF16, name="h2g", tag="h2g", align_bytes=64)
+            h2g[sig] = hg
+            nc.vector.tensor_copy(out=hg[:], in_=h2b[sig][:].rearrange("p t n -> p n t"))
+
+        def q2(sig):
+            s, cg = divmod(sig, 3)
+            if cg == 0:
+                a = p_h2c.tile([P, 3, BLK], U32, name="h2c", tag="h2c", align_bytes=64)
+                b = p_h2c.tile([P, 3, BLK], U8, name="h2s", tag="h2s", align_bytes=64)
+                h2c[s] = a
+                h2s[s] = b
+            nc.vector.quantize_mx(
+                out=h2c[s][:, cg, :].bitcast(FP8X4), scales=h2s[s][:, cg, :],
+                in_=h2g[sig][:].rearrange("p n t -> p (n t)"),
+            )
+
+        def m2(s, a):
+            e = s // NBLK
+            ps = ps_m2.tile([P, 512], F32, name="m2", tag="m2")
+            m2t[(s, a)] = ps
+            for (lo, hi) in ((0, 256), (256, 384)):
+                for cg in range(3):
+                    nc.tensor.matmul_mx(
+                        out=ps[:, lo:hi],
+                        lhsT=h2c[s][:, cg, P * a:P * (a + 1)].bitcast(FP8X4),
+                        lhsT_scale=h2s[s][:, cg, P * a:P * (a + 1)],
+                        rhs=w3c[e][:, cg, lo:hi].bitcast(FP8X4),
+                        rhs_scale=w3s[e][:, cg, lo:hi],
+                        start=(cg == 0),
+                        stop=(cg == 2),
+                    )
+
+        def e3(s, a):
+            e, nb = divmod(s, NBLK)
+            prev = b3m[:] if e == 0 else acc[:, nb, a, :]
+            nc.vector.scalar_tensor_tensor(
+                out=acc[:, nb, a, :], in0=m2t[(s, a)][:, 0:DO], scalar=1.0 / TREES, in1=prev,
+                op0=ALU.mult, op1=ALU.add,
+            )
+            if e == TREES - 1:
+                rows = out[nb * BLK:(nb + 1) * BLK, :].rearrange("(r a) c -> r a c", a=4)
+                if nb == NBLK - 1:
+                    nc.sync.dma_start(out=rows[:, a, :], in_=acc[:, nb, a, :])
+                elif a == 3:
+                    nc.sync.dma_start(out=rows, in_=acc[:, nb, :, :])
+
+        def vector_slot(sig):
+            q1s = tr_of_slot(sig - 1)
+            if sig > 0:
+                for tau in q1s:
+                    q1(tau)
+            if 1 <= sig <= SLOTS:
+                i2(sig - 1)
+            for (s, a) in m2_of_slot(sig - 1):
+                e3(s, a)
+            need_q2 = 1 <= sig <= SLOTS
+            pend = [(e, i) for (e, i, urgent) in units_of_slot(sig - 1) if not urgent]
+            k = 0
+            for (e, i, urgent) in units_of_slot(sig):
+                if urgent:
+                    wc_s((e, i))
+                wc_v((e, i))
+                if sig == 0 and k < 3:
+                    q1(q1s[k])
+                k += 1
+                if need_q2:
+                    q2(sig - 1)
+                    need_q2 = False
+                elif len(pend) > 0:
+                    wq(pend.pop(0))
+                if urgent:
+                    pend.append((e, i))
+            if need_q2:
+                q2(sig - 1)
+            for u in pend:
+                wq(u)
+
+        def loads_of_slot(sig):
+            if sig == 0:
+                for i in range(6, 9):
+                    load_w2(0, i)
+                load_h1(2)
+                load_w3(0)
+            if (sig + 7) % 3 == 0 and 3 <= (sig + 7) // 3 < STEPS:
+                load_h1((sig + 7) // 3)
+            for (e, i, urgent) in units_of_slot(sig + 2):
+                if not urgent and i < 9:
+                    load_w2(e, i)
+                if not urgent and i == 9:
+                    load_w3(e)
+            if sig % 12 == 5 and sig // 12 + 1 < TREES:
+                load_b2(sig // 12 + 1)
+
+        nc.vector.memset(warm[:], 0.0)
+        nc.scalar.activation(out=warm[:, 0:1], in_=warm[:, 1:2], func=ACT.Relu)
+        masks.make_identity(nc, ident[:])
+        nc.vector.memset(ones[:], 1.0)
+        nc.vector.memset(b3pad[:], 0.0)
+        load_h1(0)
+        for i in range(3):
+            load_w2(0, i)
+        load_b2(0)
+        nc.sync.dma_start(out=b3pad[0:TREES, 0:DO], in_=b3[:, :])
+        for i in range(3, 6):
+            load_w2(0, i)
+        load_h1(1)
+        for tau in tr_of_slot(-1):
+            tr_run(tau)
+        bsum = ps_m2.tile([P, 512], F32, name="m2", tag="m2")
+
+        for sig in range(SLOTS + 1):
+            if sig == 2:
+                nc.vector.tensor_scalar_mul(out=b3m[:], in0=bsum[:, 0:DO], scalar1=1.0 / TREES)
+            vector_slot(sig)
+            if sig < SLOTS:
+                m1(sig)
+                for tau in tr_of_slot(sig):
+                    tr_run(tau)
+                if sig == 0:
+                    nc.tensor.matmul(out=bsum[:], lhsT=ones[:], rhs=b3pad[:], start=True, stop=True)
+                for (s, a) in m2_of_slot(sig):
+                    m2(s, a)
+                for (e, i, urgent) in units_of_slot(sig):
+                    if not urgent:
+                        wc_s((e, i))
+                loads_of_slot(sig)
+        for a in range(4):
+            m2(STEPS - 1, a)
+            e3(STEPS - 1, a)

@@ -19,9 +19,10 @@ BLK = 512
 NBLK = TOK // BLK
 STEPS = TREES * NBLK
 SLOTS = 3 * STEPS
-M0 = 80
-C0 = 240
-PRESORT = False
+M0 = 64
+C0 = 192
+PRESORT = True
+PS_LEAD = 5
 
 
 def m2_of_slot(sig):
@@ -41,6 +42,16 @@ def tr_of_slot(sig):
     if sig + 4 < SLOTS:
         return [sig + 4]
     return []
+
+
+def ps_of_slot(sig):
+    if sig < 1:
+        return []
+    if sig == 1:
+        return [3, 4, 5]
+    if sig == 2:
+        return [6, 7]
+    return tr_of_slot(sig + 1)
 
 
 def units_of_slot(sig):
@@ -65,6 +76,7 @@ def tile_randomforestmlp_pa_l_kernel(tc, h1, W2, b2, W3, b3, out):
     with ExitStack() as ctx:
         const = ctx.enter_context(tc.tile_pool(name="const", bufs=1))
         p_h1raw = ctx.enter_context(tc.tile_pool(name="h1raw", bufs=2))
+        p_srt = ctx.enter_context(tc.tile_pool(name="srt", bufs=3))
         p_h1g = ctx.enter_context(tc.tile_pool(name="h1g", bufs=3))
         p_h1c = ctx.enter_context(tc.tile_pool(name="h1c", bufs=2))
         p_wraw = ctx.enter_context(tc.tile_pool(name="wraw", bufs=6))
@@ -88,6 +100,7 @@ def tile_randomforestmlp_pa_l_kernel(tc, h1, W2, b2, W3, b3, out):
         acc = const.tile([P, NBLK, 4, DO], F32, name="acc", tag="acc")
 
         h1raw = {}
+        srt = {}
         h1g = {}
         h1c = {}
         h1s = {}
@@ -133,9 +146,17 @@ def tile_randomforestmlp_pa_l_kernel(tc, h1, W2, b2, W3, b3, out):
                 in_=b2[e, :].rearrange("(c p t) -> p c t", c=3, t=4),
             )
 
-        def tr_run(tau):
+        def presort(tau):
             s, g = divmod(tau, 3)
             words = h1raw[s][:].bitcast(F32)
+            st = p_srt.tile([P, 4, 2, P], F32, name="srt", tag="srt")
+            srt[tau] = st
+            nc.vector.tensor_copy(
+                out=st[:], in_=words[:, :, 256 * g:256 * (g + 1)].rearrange("p a (j u) -> p a u j", u=2)
+            )
+
+        def tr_run(tau):
+            s, g = divmod(tau, 3)
             hg = p_h1g.tile([P, 2048], BF16, name="h1g", tag="h1g", align_bytes=64)
             h1g[tau] = hg
             hgw = hg[:].bitcast(F32)
@@ -144,7 +165,7 @@ def tile_randomforestmlp_pa_l_kernel(tc, h1, W2, b2, W3, b3, out):
                 for a2 in range(2):
                     for u in range(2):
                         nc.tensor.transpose(
-                            tp[:, a2, u, :], words[:, 2 * b + a2, 256 * g + u:256 * (g + 1):2], ident[:]
+                            tp[:, a2, u, :], srt[tau][:, 2 * b + a2, u, :], ident[:]
                         )
                 nc.scalar.copy(
                     out=hgw[:, 512 * b:512 * (b + 1)].rearrange("p (a r u) -> p a r u", a=2, u=2),
@@ -288,6 +309,8 @@ def tile_randomforestmlp_pa_l_kernel(tc, h1, W2, b2, W3, b3, out):
             if sig > 0:
                 for tau in q1s:
                     q1(tau)
+            for tau in ps_of_slot(sig):
+                presort(tau)
             if 1 <= sig <= SLOTS:
                 i2(sig - 1)
             for (s, a) in m2_of_slot(sig - 1):
@@ -320,8 +343,8 @@ def tile_randomforestmlp_pa_l_kernel(tc, h1, W2, b2, W3, b3, out):
                     load_w2(0, i)
                 load_h1(2)
                 load_w3(0)
-            if (sig + 7) % 3 == 0 and 3 <= (sig + 7) // 3 < STEPS:
-                load_h1((sig + 7) // 3)
+            if (sig + 8) % 3 == 0 and 3 <= (sig + 8) // 3 < STEPS:
+                load_h1((sig + 8) // 3)
             for (e, i, urgent) in units_of_slot(sig + 2):
                 if not urgent and i < 9:
                     load_w2(e, i)
@@ -344,7 +367,10 @@ def tile_randomforestmlp_pa_l_kernel(tc, h1, W2, b2, W3, b3, out):
             load_w2(0, i)
         load_h1(1)
         for tau in tr_of_slot(-1):
+            presort(tau)
             tr_run(tau)
+        for tau in ps_of_slot(-1):
+            presort(tau)
         bsum = ps_m2.tile([P, 512], F32, name="m2", tag="m2")
 
         for sig in range(SLOTS + 1):

@@ -21,37 +21,55 @@ STEPS = TREES * NBLK
 SLOTS = 3 * STEPS
 M0 = 64
 C0 = 192
-PRESORT = True
-PS_LEAD = 5
+M0U = 80
+PS_G = (0, 1)
+GOUTER = 0
+
+
+def runs_of_slot(sig):
+    s, cg = divmod(sig, 3)
+    if sig == -1:
+        return [(0, (0, 1, 2)), (0, (3, 4, 5))]
+    if sig == 0:
+        return []
+    if sig == 1:
+        return [(1, (0, 1, 2)), (1, (3, 4, 5))]
+    if cg == 2 and s + 2 < STEPS:
+        return [(s + 2, (0, 1, 2))]
+    if cg == 0 and s + 1 < STEPS:
+        return [(s + 1, (3, 4, 5))]
+    return []
+
+
+def q1_of_slot(sig):
+    res = []
+    for (s, banks) in runs_of_slot(sig - 1):
+        if banks[0] == 0:
+            res.append((s, 0))
+        else:
+            res.append((s, 1))
+            res.append((s, 2))
+    return res
+
+
+def sorted_first(s, g):
+    return g in PS_G and s >= 3
+
+
+def ps_of_slot(sig):
+    s, g = divmod(sig, 3)
+    if sig >= 0 and s + 2 < STEPS and sorted_first(s + 2, g):
+        return [(s + 2, g)]
+    return []
 
 
 def m2_of_slot(sig):
     s, cg = divmod(sig, 3)
-    if sig < 3 or sig >= SLOTS or cg == 0:
+    if sig < 3 or sig >= SLOTS:
         return []
-    return [(s - 1, 2 * cg - 2), (s - 1, 2 * cg - 1)]
-
-
-def tr_of_slot(sig):
-    if sig == -1:
-        return [0, 1, 2]
-    if sig == 0:
-        return []
-    if sig == 1:
-        return [3, 4, 5]
-    if sig + 4 < SLOTS:
-        return [sig + 4]
-    return []
-
-
-def ps_of_slot(sig):
-    if sig < 1:
-        return []
-    if sig == 1:
-        return [3, 4, 5]
-    if sig == 2:
-        return [6, 7]
-    return tr_of_slot(sig + 1)
+    if s == STEPS - 1:
+        return [(s - 1, a) for a in range(4)] if cg == 2 else []
+    return [(s - 1, a) for a in range(4)] if cg == 1 else []
 
 
 def units_of_slot(sig):
@@ -86,9 +104,8 @@ def tile_randomforestmlp_pa_l_kernel(tc, h1, W2, b2, W3, b3, out):
         p_h2b = ctx.enter_context(tc.tile_pool(name="h2b", bufs=3))
         p_h2g = ctx.enter_context(tc.tile_pool(name="h2g", bufs=2))
         p_h2c = ctx.enter_context(tc.tile_pool(name="h2c", bufs=2))
-        ps_m1 = ctx.enter_context(tc.psum_pool(name="psm1", bufs=4))
-        ps_tp = ctx.enter_context(tc.psum_pool(name="pstp", bufs=2))
-        ps_m2 = ctx.enter_context(tc.psum_pool(name="psm2", bufs=2))
+        ps_acc = ctx.enter_context(tc.psum_pool(name="psacc", bufs=5))
+        ps_tp = ctx.enter_context(tc.psum_pool(name="pstp", bufs=3))
         ctx.enter_context(tc.manual_schedule())
 
         ident = const.tile([P, P], F32, name="ident", tag="ident")
@@ -121,7 +138,12 @@ def tile_randomforestmlp_pa_l_kernel(tc, h1, W2, b2, W3, b3, out):
             e, nb = divmod(s, NBLK)
             t = p_h1raw.tile([P, 4, DH], BF16, name="h1raw", tag="h1raw")
             h1raw[s] = t
-            nc.sync.dma_start(out=t[:], in_=h1[e, nb * BLK:(nb + 1) * BLK, :].rearrange("(p a) k -> p a k", a=4))
+            rows = h1[e, nb * BLK:(nb + 1) * BLK, :].rearrange("(p a) k -> p a k", a=4)
+            if s == 0:
+                for g in range(3):
+                    nc.sync.dma_start(out=t[:, :, 512 * g:512 * (g + 1)], in_=rows[:, :, 512 * g:512 * (g + 1)])
+            else:
+                nc.sync.dma_start(out=t[:], in_=rows)
 
         def load_w2(e, i):
             cg, g = divmod(i, 3)
@@ -146,40 +168,40 @@ def tile_randomforestmlp_pa_l_kernel(tc, h1, W2, b2, W3, b3, out):
                 in_=b2[e, :].rearrange("(c p t) -> p c t", c=3, t=4),
             )
 
-        def presort(tau):
-            s, g = divmod(tau, 3)
+        def presort(s, g):
             words = h1raw[s][:].bitcast(F32)
             st = p_srt.tile([P, 4, 2, P], F32, name="srt", tag="srt")
-            srt[tau] = st
+            srt[(s, g)] = st
             nc.vector.tensor_copy(
                 out=st[:], in_=words[:, :, 256 * g:256 * (g + 1)].rearrange("p a (j u) -> p a u j", u=2)
             )
 
-        def tr_run(tau):
-            s, g = divmod(tau, 3)
-            hg = p_h1g.tile([P, 2048], BF16, name="h1g", tag="h1g", align_bytes=64)
-            h1g[tau] = hg
-            hgw = hg[:].bitcast(F32)
-            for b in range(2):
-                tp = ps_tp.tile([P, 2, 2, P], F32, name="tp", tag="tp")
-                for a2 in range(2):
-                    for u in range(2):
-                        nc.tensor.transpose(
-                            tp[:, a2, u, :], srt[tau][:, 2 * b + a2, u, :], ident[:]
-                        )
-                nc.scalar.copy(
-                    out=hgw[:, 512 * b:512 * (b + 1)].rearrange("p (a r u) -> p a r u", a=2, u=2),
-                    in_=tp[:].rearrange("p a u r -> p a r u"),
-                )
+        def tr_bank(s, bank):
+            g, b = divmod(bank, 2)
+            if b == 0:
+                hg = p_h1g.tile([P, 2048], BF16, name="h1g", tag="h1g", align_bytes=64)
+                h1g[(s, g)] = hg
+            hgw = h1g[(s, g)][:].bitcast(F32)
+            tp = ps_tp.tile([P, 2, 2, P], F32, name="tp", tag="tp")
+            for a2 in range(2):
+                for u in range(2):
+                    if (s, g) in srt:
+                        src = srt[(s, g)][:, 2 * b + a2, u, :]
+                    else:
+                        src = h1raw[s][:].bitcast(F32)[:, 2 * b + a2, 256 * g + u:256 * (g + 1):2]
+                    nc.tensor.transpose(tp[:, a2, u, :], src, ident[:])
+            nc.scalar.copy(
+                out=hgw[:, 512 * b:512 * (b + 1)].rearrange("p (a r u) -> p a r u", a=2, u=2),
+                in_=tp[:].rearrange("p a u r -> p a r u"),
+            )
 
-        def q1(tau):
-            s, g = divmod(tau, 3)
+        def q1(s, g):
             if g == 0:
                 hc = p_h1c.tile([P, 3, BLK], U32, name="h1c", tag="h1c", align_bytes=64)
                 hs = p_h1c.tile([P, 3, BLK], U8, name="h1s", tag="h1s", align_bytes=64)
                 h1c[s] = hc
                 h1s[s] = hs
-            nc.vector.quantize_mx(out=h1c[s][:, g, :].bitcast(FP8X4), scales=h1s[s][:, g, :], in_=h1g[tau][:])
+            nc.vector.quantize_mx(out=h1c[s][:, g, :].bitcast(FP8X4), scales=h1s[s][:, g, :], in_=h1g[(s, g)][:])
 
         def wg_of(u):
             if u not in wg:
@@ -191,9 +213,10 @@ def tile_randomforestmlp_pa_l_kernel(tc, h1, W2, b2, W3, b3, out):
             e, i = u
             t = wg_of(u)
             if i < 9:
+                m0 = M0U if e == 0 else M0
                 dst = t[:].rearrange("p (t m j) -> p t m j", t=4, j=4)
                 src = wraw[u][:].rearrange("p j (m t) -> p t m j", t=4)
-                return (dst[:, :, 0:M0, :], src[:, :, 0:M0, :], dst[:, :, M0:P, :], src[:, :, M0:P, :])
+                return (dst[:, :, 0:m0, :], src[:, :, 0:m0, :], dst[:, :, m0:P, :], src[:, :, m0:P, :])
             dst = t[:, 0:4 * DO].rearrange("p (c j) -> p c j", j=4)
             src = w3raw[e][:, i - 9, :, :].rearrange("p j c -> p c j")
             return (dst[:, 0:C0, :], src[:, 0:C0, :], dst[:, C0:DO, :], src[:, C0:DO, :])
@@ -239,23 +262,29 @@ def tile_randomforestmlp_pa_l_kernel(tc, h1, W2, b2, W3, b3, out):
             e = s // NBLK
             hb = p_h2b.tile([P, 4, BLK], BF16, name="h2b", tag="h2b")
             h2b[sig] = hb
-            for t in range(4):
-                bank = ps_m1.tile([P, BLK], F32, name="m1", tag="m1")
+            order = [(t, g) for t in range(4) for g in range(3)]
+            if sig < GOUTER:
+                order = [(t, g) for g in range(3) for t in range(4)]
+            banks = {}
+            for (t, g) in order:
+                if t not in banks:
+                    bank = ps_acc.tile([P, BLK], F32, name="acc", tag="acc")
+                    banks[t] = bank
                 c0 = 512 * cg + 128 * t
-                for g in range(3):
-                    nc.tensor.matmul_mx(
-                        out=bank[:],
-                        lhsT=w2c[e][:, g, c0:c0 + P].bitcast(FP8X4),
-                        lhsT_scale=w2s[e][:, g, c0:c0 + P],
-                        rhs=h1c[s][:, g, :].bitcast(FP8X4),
-                        rhs_scale=h1s[s][:, g, :],
-                        start=(g == 0),
-                        stop=(g == 2),
-                    )
-                nc.scalar.activation(
-                    out=hb[:, t, :], in_=bank[:], func=ACT.Relu,
-                    bias=b2t[:, e, 4 * cg + t:4 * cg + t + 1], scale=1.0,
+                nc.tensor.matmul_mx(
+                    out=banks[t][:],
+                    lhsT=w2c[e][:, g, c0:c0 + P].bitcast(FP8X4),
+                    lhsT_scale=w2s[e][:, g, c0:c0 + P],
+                    rhs=h1c[s][:, g, :].bitcast(FP8X4),
+                    rhs_scale=h1s[s][:, g, :],
+                    start=(g == 0),
+                    stop=(g == 2),
                 )
+                if g == 2:
+                    nc.scalar.activation(
+                        out=hb[:, t, :], in_=banks[t][:], func=ACT.Relu,
+                        bias=b2t[:, e, 4 * cg + t:4 * cg + t + 1], scale=1.0,
+                    )
 
         def i2(sig):
             hg = p_h2g.tile([P, BLK, 4], BF16, name="h2g", tag="h2g", align_bytes=64)
@@ -276,7 +305,7 @@ def tile_randomforestmlp_pa_l_kernel(tc, h1, W2, b2, W3, b3, out):
 
         def m2(s, a):
             e = s // NBLK
-            ps = ps_m2.tile([P, 512], F32, name="m2", tag="m2")
+            ps = ps_acc.tile([P, BLK], F32, name="acc", tag="acc")
             m2t[(s, a)] = ps
             for (lo, hi) in ((0, 256), (256, 384)):
                 for cg in range(3):
@@ -305,16 +334,19 @@ def tile_randomforestmlp_pa_l_kernel(tc, h1, W2, b2, W3, b3, out):
                     nc.sync.dma_start(out=rows, in_=acc[:, nb, :, :])
 
         def vector_slot(sig):
-            q1s = tr_of_slot(sig - 1)
-            if sig > 0:
-                for tau in q1s:
-                    q1(tau)
-            for tau in ps_of_slot(sig):
-                presort(tau)
+            q1s = q1_of_slot(sig)
+            late_e3 = []
+            if sig < SLOTS:
+                for (s, a) in m2_of_slot(sig - 1):
+                    e3(s, a)
             if 1 <= sig <= SLOTS:
                 i2(sig - 1)
-            for (s, a) in m2_of_slot(sig - 1):
-                e3(s, a)
+            if sig == SLOTS:
+                late_e3 = m2_of_slot(sig - 1)
+                e3(late_e3[0][0], late_e3[0][1])
+                late_e3 = late_e3[1:]
+            for (s, g) in ps_of_slot(sig):
+                presort(s, g)
             need_q2 = 1 <= sig <= SLOTS
             pend = [(e, i) for (e, i, urgent) in units_of_slot(sig - 1) if not urgent]
             k = 0
@@ -323,7 +355,7 @@ def tile_randomforestmlp_pa_l_kernel(tc, h1, W2, b2, W3, b3, out):
                     wc_s((e, i))
                 wc_v((e, i))
                 if sig == 0 and k < 3:
-                    q1(q1s[k])
+                    q1(q1s[k][0], q1s[k][1])
                 k += 1
                 if need_q2:
                     q2(sig - 1)
@@ -336,6 +368,11 @@ def tile_randomforestmlp_pa_l_kernel(tc, h1, W2, b2, W3, b3, out):
                 q2(sig - 1)
             for u in pend:
                 wq(u)
+            if sig > 0:
+                for (s, g) in q1s:
+                    q1(s, g)
+            for (s, a) in late_e3:
+                e3(s, a)
 
         def loads_of_slot(sig):
             if sig == 0:
@@ -343,8 +380,10 @@ def tile_randomforestmlp_pa_l_kernel(tc, h1, W2, b2, W3, b3, out):
                     load_w2(0, i)
                 load_h1(2)
                 load_w3(0)
-            if (sig + 8) % 3 == 0 and 3 <= (sig + 8) // 3 < STEPS:
-                load_h1((sig + 8) // 3)
+            if sig == 1:
+                load_h1(3)
+            if sig >= 3 and sig % 3 == 0 and sig // 3 + 3 < STEPS:
+                load_h1(sig // 3 + 3)
             for (e, i, urgent) in units_of_slot(sig + 2):
                 if not urgent and i < 9:
                     load_w2(e, i)
@@ -366,25 +405,24 @@ def tile_randomforestmlp_pa_l_kernel(tc, h1, W2, b2, W3, b3, out):
         for i in range(3, 6):
             load_w2(0, i)
         load_h1(1)
-        for tau in tr_of_slot(-1):
-            presort(tau)
-            tr_run(tau)
-        for tau in ps_of_slot(-1):
-            presort(tau)
-        bsum = ps_m2.tile([P, 512], F32, name="m2", tag="m2")
+        for (s, banks) in runs_of_slot(-1):
+            for bank in banks:
+                tr_bank(s, bank)
+        bsum = ps_acc.tile([P, BLK], F32, name="acc", tag="acc")
 
         for sig in range(SLOTS + 1):
-            if sig == 2:
+            if sig == 1:
                 nc.vector.tensor_scalar_mul(out=b3m[:], in0=bsum[:, 0:DO], scalar1=1.0 / TREES)
             vector_slot(sig)
             if sig < SLOTS:
-                m1(sig)
-                for tau in tr_of_slot(sig):
-                    tr_run(tau)
                 if sig == 0:
                     nc.tensor.matmul(out=bsum[:], lhsT=ones[:], rhs=b3pad[:], start=True, stop=True)
+                m1(sig)
                 for (s, a) in m2_of_slot(sig):
                     m2(s, a)
+                for (s, banks) in runs_of_slot(sig):
+                    for bank in banks:
+                        tr_bank(s, bank)
                 for (e, i, urgent) in units_of_slot(sig):
                     if not urgent:
                         wc_s((e, i))

@@ -19,10 +19,10 @@ BLK = 512
 NBLK = TOK // BLK
 STEPS = TREES * NBLK
 SLOTS = 3 * STEPS
-M0 = 64
-C0 = 192
+M0 = 80
+C0 = 240
 M0U = 80
-PS_G = (0, 1)
+PS_G = ()
 GOUTER = 0
 
 
@@ -69,7 +69,11 @@ def m2_of_slot(sig):
         return []
     if s == STEPS - 1:
         return [(s - 1, a) for a in range(4)] if cg == 2 else []
-    return [(s - 1, a) for a in range(4)] if cg == 1 else []
+    if cg == 1:
+        return [(s - 1, 0), (s - 1, 1), (s - 1, 2)]
+    if cg == 2:
+        return [(s - 1, 3)]
+    return []
 
 
 def units_of_slot(sig):
@@ -94,7 +98,6 @@ def tile_randomforestmlp_pa_l_kernel(tc, h1, W2, b2, W3, b3, out):
     with ExitStack() as ctx:
         const = ctx.enter_context(tc.tile_pool(name="const", bufs=1))
         p_h1raw = ctx.enter_context(tc.tile_pool(name="h1raw", bufs=2))
-        p_srt = ctx.enter_context(tc.tile_pool(name="srt", bufs=3))
         p_h1g = ctx.enter_context(tc.tile_pool(name="h1g", bufs=3))
         p_h1c = ctx.enter_context(tc.tile_pool(name="h1c", bufs=2))
         p_wraw = ctx.enter_context(tc.tile_pool(name="wraw", bufs=6))
@@ -104,8 +107,8 @@ def tile_randomforestmlp_pa_l_kernel(tc, h1, W2, b2, W3, b3, out):
         p_h2b = ctx.enter_context(tc.tile_pool(name="h2b", bufs=3))
         p_h2g = ctx.enter_context(tc.tile_pool(name="h2g", bufs=2))
         p_h2c = ctx.enter_context(tc.tile_pool(name="h2c", bufs=2))
-        ps_acc = ctx.enter_context(tc.psum_pool(name="psacc", bufs=5))
-        ps_tp = ctx.enter_context(tc.psum_pool(name="pstp", bufs=3))
+        ps_acc = ctx.enter_context(tc.psum_pool(name="psacc", bufs=4))
+        ps_tp = ctx.enter_context(tc.psum_pool(name="psaux", bufs=4))
         ctx.enter_context(tc.manual_schedule())
 
         ident = const.tile([P, P], F32, name="ident", tag="ident")
@@ -166,14 +169,6 @@ def tile_randomforestmlp_pa_l_kernel(tc, h1, W2, b2, W3, b3, out):
             nc.sync.dma_start(
                 out=b2t[:, e, 0:12].rearrange("p (c t) -> p c t", t=4),
                 in_=b2[e, :].rearrange("(c p t) -> p c t", c=3, t=4),
-            )
-
-        def presort(s, g):
-            words = h1raw[s][:].bitcast(F32)
-            st = p_srt.tile([P, 4, 2, P], F32, name="srt", tag="srt")
-            srt[(s, g)] = st
-            nc.vector.tensor_copy(
-                out=st[:], in_=words[:, :, 256 * g:256 * (g + 1)].rearrange("p a (j u) -> p a u j", u=2)
             )
 
         def tr_bank(s, bank):
@@ -305,7 +300,7 @@ def tile_randomforestmlp_pa_l_kernel(tc, h1, W2, b2, W3, b3, out):
 
         def m2(s, a):
             e = s // NBLK
-            ps = ps_acc.tile([P, BLK], F32, name="acc", tag="acc")
+            ps = ps_tp.tile([P, BLK], F32, name="tp", tag="tp")
             m2t[(s, a)] = ps
             for (lo, hi) in ((0, 256), (256, 384)):
                 for cg in range(3):
@@ -345,8 +340,6 @@ def tile_randomforestmlp_pa_l_kernel(tc, h1, W2, b2, W3, b3, out):
                 late_e3 = m2_of_slot(sig - 1)
                 e3(late_e3[0][0], late_e3[0][1])
                 late_e3 = late_e3[1:]
-            for (s, g) in ps_of_slot(sig):
-                presort(s, g)
             need_q2 = 1 <= sig <= SLOTS
             pend = [(e, i) for (e, i, urgent) in units_of_slot(sig - 1) if not urgent]
             k = 0
@@ -408,7 +401,7 @@ def tile_randomforestmlp_pa_l_kernel(tc, h1, W2, b2, W3, b3, out):
         for (s, banks) in runs_of_slot(-1):
             for bank in banks:
                 tr_bank(s, bank)
-        bsum = ps_acc.tile([P, BLK], F32, name="acc", tag="acc")
+        bsum = ps_tp.tile([P, BLK], F32, name="tp", tag="tp")
 
         for sig in range(SLOTS + 1):
             if sig == 1:
@@ -418,11 +411,11 @@ def tile_randomforestmlp_pa_l_kernel(tc, h1, W2, b2, W3, b3, out):
                 if sig == 0:
                     nc.tensor.matmul(out=bsum[:], lhsT=ones[:], rhs=b3pad[:], start=True, stop=True)
                 m1(sig)
-                for (s, a) in m2_of_slot(sig):
-                    m2(s, a)
                 for (s, banks) in runs_of_slot(sig):
                     for bank in banks:
                         tr_bank(s, bank)
+                for (s, a) in m2_of_slot(sig):
+                    m2(s, a)
                 for (e, i, urgent) in units_of_slot(sig):
                     if not urgent:
                         wc_s((e, i))

from contextlib import ExitStack

import concourse.masks as masks
import concourse.mybir as mybir

TREES, TOK, DH, DK, DO = 8, 2048, 1536, 1536, 384
FLOPS = 2 * TREES * TOK * (DH * DK + DK * DO)

F32 = mybir.dt.float32
BF16 = mybir.dt.bfloat16
U32 = mybir.dt.uint32
U8 = mybir.dt.uint8
FP8X4 = mybir.dt.float8_e4m3fn_x4
ACT = mybir.ActivationFunctionType
ALU = mybir.AluOpType

P = 128
BLK = 512
NBLK = TOK // BLK
STEPS = TREES * NBLK
SLOTS = 3 * STEPS
M0 = 80
C0 = 240
M0U = 80
PS_G = ()
GOUTER = 0


def runs_of_slot(sig):
    s, cg = divmod(sig, 3)
    if sig == -1:
        return [(0, (0, 1, 2)), (0, (3, 4, 5))]
    if sig == 0:
        return []
    if sig == 1:
        return [(1, (0, 1, 2)), (1, (3, 4, 5))]
    if cg == 2 and s + 2 < STEPS:
        return [(s + 2, (0, 1, 2))]
    if cg == 0 and s + 1 < STEPS:
        return [(s + 1, (3, 4, 5))]
    return []


def q1_of_slot(sig):
    res = []
    for (s, banks) in runs_of_slot(sig - 1):
        if banks[0] == 0:
            res.append((s, 0))
        else:
            res.append((s, 1))
            res.append((s, 2))
    return res


def sorted_first(s, g):
    return g in PS_G and s >= 3


def ps_of_slot(sig):
    s, g = divmod(sig, 3)
    if sig >= 0 and s + 2 < STEPS and sorted_first(s + 2, g):
        return [(s + 2, g)]
    return []


def m2_of_slot(sig):
    s, cg = divmod(sig, 3)
    if sig < 3 or sig >= SLOTS:
        return []
    if s == STEPS - 1:
        return [(s - 1, a) for a in range(4)] if cg == 2 else []
    if cg == 1:
        return [(s - 1, 0), (s - 1, 1), (s - 1, 2)]
    if cg == 2:
        return [(s - 1, 3)]
    return []


def units_of_slot(sig):
    if sig < 0:
        return []
    if sig == 0:
        return [(0, i, True) for i in range(6)]
    if sig == 1:
        return [(0, i, True) for i in range(6, 9)]
    if sig == 2:
        return [(0, i, True) for i in range(9, 12)]
    if sig < 6:
        return [(1, 2 * (sig - 3), False), (1, 2 * (sig - 3) + 1, False)]
    e, i = divmod(sig, 12)
    if e + 1 < TREES:
        return [(e + 1, i, False)]
    return []


def tile_randomforestmlp_pa_l_kernel(tc, h1, W2, b2, W3, b3, out):
    nc = tc.nc
    with ExitStack() as ctx:
        const = ctx.enter_context(tc.tile_pool(name="const", bufs=1))
        p_h1raw = ctx.enter_context(tc.tile_pool(name="h1raw", bufs=2))
        p_h1g = ctx.enter_context(tc.tile_pool(name="h1g", bufs=3))
        p_h1c = ctx.enter_context(tc.tile_pool(name="h1c", bufs=2))
        p_wraw = ctx.enter_context(tc.tile_pool(name="wraw", bufs=6))
        p_w3raw = ctx.enter_context(tc.tile_pool(name="w3raw", bufs=1))
        p_wg = ctx.enter_context(tc.tile_pool(name="wg", bufs=4))
        p_wc = ctx.enter_context(tc.tile_pool(name="wc", bufs=2))
        p_h2b = ctx.enter_context(tc.tile_pool(name="h2b", bufs=3))
        p_h2g = ctx.enter_context(tc.tile_pool(name="h2g", bufs=2))
        p_h2c = ctx.enter_context(tc.tile_pool(name="h2c", bufs=2))
        ps_acc = ctx.enter_context(tc.psum_pool(name="psacc", bufs=4))
        ps_tp = ctx.enter_context(tc.psum_pool(name="psaux", bufs=4))
        ctx.enter_context(tc.manual_schedule())

        ident = const.tile([P, P], F32, name="ident", tag="ident")
        ones = const.tile([P, P], BF16, name="ones", tag="ones")
        b3pad = const.tile([P, 512], BF16, name="b3pad", tag="b3pad")
        b3m = const.tile([P, DO], F32, name="b3m", tag="b3m")
        b2t = const.tile([P, TREES, 16], BF16, name="b2t", tag="b2t")
        warm = const.tile([P, 8], F32, name="warm", tag="warm")
        acc = const.tile([P, NBLK, 4, DO], F32, name="acc", tag="acc")

        h1raw = {}
        srt = {}
        h1g = {}
        h1c = {}
        h1s = {}
        wraw = {}
        w3raw = {}
        wg = {}
        w2c = {}
        w2s = {}
        w3c = {}
        w3s = {}
        h2b = {}
        h2g = {}
        h2c = {}
        h2s = {}
        m2t = {}

        def load_h1(s):
            e, nb = divmod(s, NBLK)
            t = p_h1raw.tile([P, 4, DH], BF16, name="h1raw", tag="h1raw")
            h1raw[s] = t
            rows = h1[e, nb * BLK:(nb + 1) * BLK, :].rearrange("(p a) k -> p a k", a=4)
            if s == 0:
                for g in range(3):
                    nc.sync.dma_start(out=t[:, :, 512 * g:512 * (g + 1)], in_=rows[:, :, 512 * g:512 * (g + 1)])
            else:
                nc.sync.dma_start(out=t[:], in_=rows)

        def load_w2(e, i):
            cg, g = divmod(i, 3)
            t = p_wraw.tile([P, 4, 512], BF16, name="wraw", tag="wraw")
            wraw[(e, i)] = t
            nc.sync.dma_start(
                out=t[:],
                in_=W2[e, 512 * g:512 * (g + 1), 512 * cg:512 * (cg + 1)].rearrange("(p j) c -> p j c", j=4),
            )

        def load_w3(e):
            t = p_w3raw.tile([P, 3, 4, DO], BF16, name="w3raw", tag="w3raw")
            w3raw[e] = t
            nc.sync.dma_start(
                out=t[:].rearrange("p g j c -> p g (j c)"),
                in_=W3[e, :, :].rearrange("(g p j) c -> p g (j c)", g=3, j=4),
            )

        def load_b2(e):
            nc.sync.dma_start(
                out=b2t[:, e, 0:12].rearrange("p (c t) -> p c t", t=4),
                in_=b2[e, :].rearrange("(c p t) -> p c t", c=3, t=4),
            )

        def tr_bank(s, bank):
            g, b = divmod(bank, 2)
            if b == 0:
                hg = p_h1g.tile([P, 2048], BF16, name="h1g", tag="h1g", align_bytes=64)
                h1g[(s, g)] = hg
            hgw = h1g[(s, g)][:].bitcast(F32)
            tp = ps_tp.tile([P, 2, 2, P], F32, name="tp", tag="tp")
            for a2 in range(2):
                for u in range(2):
                    if (s, g) in srt:
                        src = srt[(s, g)][:, 2 * b + a2, u, :]
                    else:
                        src = h1raw[s][:].bitcast(F32)[:, 2 * b + a2, 256 * g + u:256 * (g + 1):2]
                    nc.tensor.transpose(tp[:, a2, u, :], src, ident[:])
            nc.scalar.copy(
                out=hgw[:, 512 * b:512 * (b + 1)].rearrange("p (a r u) -> p a r u", a=2, u=2),
                in_=tp[:].rearrange("p a u r -> p a r u"),
            )

        def q1(s, g):
            if g == 0:
                hc = p_h1c.tile([P, 3, BLK], U32, name="h1c", tag="h1c", align_bytes=64)
                hs = p_h1c.tile([P, 3, BLK], U8, name="h1s", tag="h1s", align_bytes=64)
                h1c[s] = hc
                h1s[s] = hs
            nc.vector.quantize_mx(out=h1c[s][:, g, :].bitcast(FP8X4), scales=h1s[s][:, g, :], in_=h1g[(s, g)][:])

        def wg_of(u):
            if u not in wg:
                t = p_wg.tile([P, 2048], BF16, name="wg", tag="wg", align_bytes=64)
                wg[u] = t
            return wg[u]

        def wc_views(u):
            e, i = u
            t = wg_of(u)
            if i < 9:
                m0 = M0U if e == 0 else M0
                dst = t[:].rearrange("p (t m j) -> p t m j", t=4, j=4)
                src = wraw[u][:].rearrange("p j (m t) -> p t m j", t=4)
                return (dst[:, :, 0:m0, :], src[:, :, 0:m0, :], dst[:, :, m0:P, :], src[:, :, m0:P, :])
            dst = t[:, 0:4 * DO].rearrange("p (c j) -> p c j", j=4)
            src = w3raw[e][:, i - 9, :, :].rearrange("p j c -> p c j")
            return (dst[:, 0:C0, :], src[:, 0:C0, :], dst[:, C0:DO, :], src[:, C0:DO, :])

        def wc_v(u):
            v = wc_views(u)
            nc.vector.tensor_copy(out=v[0], in_=v[1])

        def wc_s(u):
            v = wc_views(u)
            nc.scalar.copy(out=v[2], in_=v[3])

        def wq(u):
            e, i = u
            if i == 0:
                a = p_wc.tile([P, 3, DK], U32, name="w2c", tag="w2c", align_bytes=64)
                b = p_wc.tile([P, 3, DK], U8, name="w2s", tag="w2s", align_bytes=64)
                w2c[e] = a
                w2s[e] = b
            if i == 9:
                a = p_wc.tile([P, 3, DO], U32, name="w3c", tag="w3c", align_bytes=64)
                b = p_wc.tile([P, 3, DO], U8, name="w3s", tag="w3s", align_bytes=64)
                w3c[e] = a
                w3s[e] = b
            if i < 9:
                cg, g = divmod(i, 3)
                nc.vector.quantize_mx(
                    out=w2c[e][:, g, 512 * cg:512 * (cg + 1)].bitcast(FP8X4),
                    scales=w2s[e][:, g, 512 * cg:512 * (cg + 1)],
                    in_=wg[u][:],
                )
            else:
                g = i - 9
                for (lo, hi) in ((0, 256), (256, 384)):
                    nc.vector.quantize_mx(
                        out=w3c[e][:, g, lo:hi].bitcast(FP8X4),
                        scales=w3s[e][:, g, lo:hi],
                        in_=wg[u][:, 4 * lo:4 * hi],
                    )

        def m1(sig):
            s, cg = divmod(sig, 3)
            e = s // NBLK
            hb = p_h2b.tile([P, 4, BLK], BF16, name="h2b", tag="h2b")
            h2b[sig] = hb
            order = [(t, g) for t in range(4) for g in range(3)]
            if sig < GOUTER:
                order = [(t, g) for g in range(3) for t in range(4)]
            banks = {}
            for (t, g) in order:
                if t not in banks:
                    bank = ps_acc.tile([P, BLK], F32, name="acc", tag="acc")
                    banks[t] = bank
                c0 = 512 * cg + 128 * t
                nc.tensor.matmul_mx(
                    out=banks[t][:],
                    lhsT=w2c[e][:, g, c0:c0 + P].bitcast(FP8X4),
                    lhsT_scale=w2s[e][:, g, c0:c0 + P],
                    rhs=h1c[s][:, g, :].bitcast(FP8X4),
                    rhs_scale=h1s[s][:, g, :],
                    start=(g == 0),
                    stop=(g == 2),
                )
                if g == 2:
                    nc.scalar.activation(
                        out=hb[:, t, :], in_=banks[t][:], func=ACT.Relu,
                        bias=b2t[:, e, 4 * cg + t:4 * cg + t + 1], scale=1.0,
                    )

        def i2(sig):
            hg = p_h2g.tile([P, BLK, 4], BF16, name="h2g", tag="h2g", align_bytes=64)
            h2g[sig] = hg
            nc.vector.tensor_copy(out=hg[:], in_=h2b[sig][:].rearrange("p t n -> p n t"))

        def q2(sig):
            s, cg = divmod(sig, 3)
            if cg == 0:
                a = p_h2c.tile([P, 3, BLK], U32, name="h2c", tag="h2c", align_bytes=64)
                b = p_h2c.tile([P, 3, BLK], U8, name="h2s", tag="h2s", align_bytes=64)
                h2c[s] = a
                h2s[s] = b
            nc.vector.quantize_mx(
                out=h2c[s][:, cg, :].bitcast(FP8X4), scales=h2s[s][:, cg, :],
                in_=h2g[sig][:].rearrange("p n t -> p (n t)"),
            )

        def m2(s, a):
            e = s // NBLK
            ps = ps_tp.tile([P, BLK], F32, name="tp", tag="tp")
            m2t[(s, a)] = ps
            for (lo, hi) in ((0, 256), (256, 384)):
                for cg in range(3):
                    nc.tensor.matmul_mx(
                        out=ps[:, lo:hi],
                        lhsT=h2c[s][:, cg, P * a:P * (a + 1)].bitcast(FP8X4),
                        lhsT_scale=h2s[s][:, cg, P * a:P * (a + 1)],
                        rhs=w3c[e][:, cg, lo:hi].bitcast(FP8X4),
                        rhs_scale=w3s[e][:, cg, lo:hi],
                        start=(cg == 0),
                        stop=(cg == 2),
                    )

        def e3(s, a):
            e, nb = divmod(s, NBLK)
            prev = b3m[:] if e == 0 else acc[:, nb, a, :]
            nc.vector.scalar_tensor_tensor(
                out=acc[:, nb, a, :], in0=m2t[(s, a)][:, 0:DO], scalar=1.0 / TREES, in1=prev,
                op0=ALU.mult, op1=ALU.add,
            )
            if e == TREES - 1:
                rows = out[nb * BLK:(nb + 1) * BLK, :].rearrange("(r a) c -> r a c", a=4)
                if nb == NBLK - 1:
                    nc.sync.dma_start(out=rows[:, a, :], in_=acc[:, nb, a, :])
                elif a == 3:
                    nc.sync.dma_start(out=rows, in_=acc[:, nb, :, :])

        def vector_slot(sig):
            q1s = q1_of_slot(sig)
            late_e3 = []
            if sig < SLOTS:
                for (s, a) in m2_of_slot(sig - 1):
                    e3(s, a)
            if 1 <= sig <= SLOTS:
                i2(sig - 1)
            if sig == SLOTS:
                late_e3 = m2_of_slot(sig - 1)
                e3(late_e3[0][0], late_e3[0][1])
                late_e3 = late_e3[1:]
            need_q2 = 1 <= sig <= SLOTS
            pend = [(e, i) for (e, i, urgent) in units_of_slot(sig - 1) if not urgent]
            k = 0
            for (e, i, urgent) in units_of_slot(sig):
                if urgent:
                    wc_s((e, i))
                wc_v((e, i))
                if sig == 0 and k < 3:
                    q1(q1s[k][0], q1s[k][1])
                k += 1
                if need_q2:
                    q2(sig - 1)
                    need_q2 = False
                elif len(pend) > 0:
                    wq(pend.pop(0))
                if urgent:
                    pend.append((e, i))
            if need_q2:
                q2(sig - 1)
            for u in pend:
                wq(u)
            if sig > 0:
                for (s, g) in q1s:
                    q1(s, g)
            for (s, a) in late_e3:
                e3(s, a)

        def loads_of_slot(sig):
            if sig == 0:
                for i in range(6, 9):
                    load_w2(0, i)
                load_h1(2)
                load_w3(0)
            if sig == 1:
                load_h1(3)
            if sig >= 3 and sig % 3 == 0 and sig // 3 + 3 < STEPS:
                load_h1(sig // 3 + 3)
            for (e, i, urgent) in units_of_slot(sig + 2):
                if not urgent and i < 9:
                    load_w2(e, i)
                if not urgent and i == 9:
                    load_w3(e)
            if sig % 12 == 5 and sig // 12 + 1 < TREES:
                load_b2(sig // 12 + 1)

        nc.vector.memset(warm[:], 0.0)
        nc.scalar.activation(out=warm[:, 0:1], in_=warm[:, 1:2], func=ACT.Relu)
        masks.make_identity(nc, ident[:])
        nc.vector.memset(ones[:], 1.0)
        nc.vector.memset(b3pad[:], 0.0)
        load_h1(0)
        for i in range(3):
            load_w2(0, i)
        load_b2(0)
        nc.sync.dma_start(out=b3pad[0:TREES, 0:DO], in_=b3[:, :])
        for i in range(3, 6):
            load_w2(0, i)
        load_h1(1)
        for (s, banks) in runs_of_slot(-1):
            for bank in banks:
                tr_bank(s, bank)
        bsum = ps_tp.tile([P, BLK], F32, name="tp", tag="tp")

        for sig in range(SLOTS + 1):
            if sig == 1:
                nc.vector.tensor_scalar_mul(out=b3m[:], in0=bsum[:, 0:DO], scalar1=1.0 / TREES)
            vector_slot(sig)
            if sig < SLOTS:
                if sig == 0:
                    nc.tensor.matmul(out=bsum[:], lhsT=ones[:], rhs=b3pad[:], start=True, stop=True)
                m1(sig)
                for (s, banks) in runs_of_slot(sig):
                    for bank in banks:
                        tr_bank(s, bank)
                for (s, a) in m2_of_slot(sig):
                    m2(s, a)
                for (e, i, urgent) in units_of_slot(sig):
                    if not urgent:
                        wc_s((e, i))
                loads_of_slot(sig)
        for a in range(4):
            m2(STEPS - 1, a)
            e3(STEPS - 1, a)
